import numpy as np
import ml_dtypes


def mxq(x, axis, fmt="e4m3"):
    dtype, down = {"e4m3": (ml_dtypes.float8_e4m3fn, 7), "e5m2": (ml_dtypes.float8_e5m2, 14)}[fmt]
    v = np.moveaxis(np.asarray(x, np.float32).astype(ml_dtypes.bfloat16).astype(np.float64), axis, -1)
    blocks = v.reshape(v.shape[:-1] + (-1, 32))
    amax = np.abs(blocks).max(-1, keepdims=True)
    byte = np.maximum(np.where(amax > 0, np.frexp(amax)[1] - 1 + 127, 0) - down, 1)
    scale = np.exp2(byte - 127.0)
    codes = (blocks / scale).astype(np.float32).astype(dtype).astype(np.float64)
    return np.moveaxis((codes * scale).reshape(v.shape), -1, axis)


WIDE = False


def mx_kscale(k):
    if not WIDE:
        return np.ones(k)
    levels = np.array([10, -10, 5, -5, 0])
    a = np.random.permutation(np.resize(levels, k // 512 * 4)).reshape(k // 512, 4)
    idx = np.arange(k)
    return np.exp2(a[idx // 512, idx % 128 // 32])


BF16 = ml_dtypes.bfloat16


def bf(x):
    return np.asarray(x, np.float32).astype(BF16)


def f64(x):
    return np.asarray(x).astype(np.float64)


B, N, DIM, H, D, QB = 1, 1024, 1024, 8, 128, 512
E = H * D
RMS_EPS = 1e-12


def setup_inputs():
    s = mx_kscale(DIM)
    return {"x": bf(np.random.standard_normal((B, N, DIM))),
            "gamma": bf((1.0 + 0.1 * np.random.standard_normal(DIM)) * s),
            "w_qkv": bf(np.random.standard_normal((DIM, 3 * E)) * 1.5 / np.sqrt(DIM) / s[:, None])}


def reference(x, gamma, w_qkv):
    xf = f64(x)
    l2 = np.maximum(np.sqrt((xf * xf).sum(-1, keepdims=True)), RMS_EPS)
    normed = xf / l2 * np.sqrt(DIM) * f64(gamma)
    y = mxq(normed, 2, "e4m3") @ mxq(f64(w_qkv), 0, "e4m3")
    qkv = y.reshape(B, N, 3, H, D).transpose(2, 0, 3, 1, 4)
    return qkv[0] * D ** -0.5, qkv[1], qkv[2]

@@ -1,0 +1,222 @@
+from contextlib import ExitStack
+
+import concourse.mybir as mybir
+from concourse.masks import make_identity
+
+F32 = mybir.dt.float32
+BF16 = mybir.dt.bfloat16
+U32 = mybir.dt.uint32
+U8 = mybir.dt.uint8
+FP8X4 = mybir.dt.float8_e4m3fn_x4
+ACT = mybir.ActivationFunctionType
+ALU = mybir.AluOpType
+
+P = 128
+TOKENS = 1024
+DIM = 1024
+HEADS = 8
+HEAD_DIM = 128
+TENSORS = 3
+RMS_EPS = 1e-12
+
+PACK = 4
+HALF_PACK = PACK // 2
+PASSES = DIM // (P * PACK)
+TILES = TOKENS // P
+PAIR = 2
+PAIRS = TILES // PAIR
+CHUNK_HEADS = 2
+CHUNK = CHUNK_HEADS * HEAD_DIM
+TENSOR_COLS = HEADS * HEAD_DIM
+CHUNKS_PER_TENSOR = TENSOR_COLS // CHUNK
+CHUNKS = TENSORS * CHUNKS_PER_TENSOR
+BANK = 512
+VECTOR_EVERY = 8
+
+FLOPS = 2 * TOKENS * DIM * TENSORS * TENSOR_COLS
+
+
+def tile_ringattention_pa_kernel(tc, x, gamma, w_qkv, out_0, out_1, out_2):
+    nc = tc.nc
+
+    x_view = x.rearrange("b (p t) k -> p (b t) k", t=TILES)
+    out_views = [o.rearrange("b h (p t) d -> p (b h) (t d)", t=TILES) for o in (out_0, out_1, out_2)]
+    w_view = w_qkv.rearrange("(g p j) n -> g p j n", g=PASSES, j=PACK)
+
+    with ExitStack() as ctx:
+        const = ctx.enter_context(tc.tile_pool(name="const", bufs=1))
+        keep = ctx.enter_context(tc.tile_pool(name="keep", bufs=1))
+        work = ctx.enter_context(tc.tile_pool(name="work", bufs=3))
+        stages = ctx.enter_context(tc.tile_pool(name="stages", bufs=4))
+        psum_turn = ctx.enter_context(tc.psum_pool(name="psum_turn", bufs=2))
+        psum_acc = ctx.enter_context(tc.psum_pool(name="psum_acc", bufs=6))
+
+        gamma_in = const.tile([1, DIM], BF16)
+        nc.sync.dma_start(out=gamma_in[:], in_=gamma.rearrange("(o k) -> o k", o=1))
+
+        x_sb = keep.tile([P, TILES, DIM], BF16)
+        for a in range(PAIRS):
+            tiles = slice(PAIR * a, PAIR * (a + 1))
+            nc.sync.dma_start(out=x_sb[:, tiles, :], in_=x_view[:, tiles, :])
+
+        w_raw = []
+        for q in range(TENSORS):
+            w_raw_q = keep.tile([P, PASSES, PACK, TENSOR_COLS], BF16, name="w_raw%d" % q)
+            for g in range(PASSES):
+                nc.sync.dma_start(
+                    out=w_raw_q[:, g, :, :],
+                    in_=w_view[g, :, :, q * TENSOR_COLS : (q + 1) * TENSOR_COLS],
+                )
+            w_raw.append(w_raw_q)
+
+        ident = const.tile([P, P], F32)
+        make_identity(nc, ident[:])
+        ones = const.tile([P, P], BF16)
+        nc.vector.memset(ones[:], 1.0)
+        one_col = const.tile([P, 1], F32)
+        nc.vector.memset(one_col[:], 1.0)
+        sqrt_warm = const.tile([P, 1], F32)
+        nc.scalar.sqrt(sqrt_warm[:], one_col[:])
+
+        gamma_row = const.tile([P, DIM], BF16)
+        nc.vector.memset(gamma_row[:], 0.0)
+        nc.vector.tensor_copy(out=gamma_row[0:1, :], in_=gamma_in[:])
+        gamma_b = const.tile([P, DIM], BF16)
+        for half in range(DIM // BANK):
+            cols = slice(half * BANK, (half + 1) * BANK)
+            spread = psum_acc.tile([P, BANK], F32, tag="acc")
+            nc.tensor.matmul(out=spread[:], lhsT=ones[:], rhs=gamma_row[:, cols], start=True, stop=True)
+            nc.vector.tensor_copy(out=gamma_b[:, cols], in_=spread[:])
+
+        x_codes = keep.tile([P, TILES, PASSES * P], U32, align_bytes=64)
+        x_scales = keep.tile([P, TILES, PASSES * P], U8, align_bytes=64)
+        w_codes = keep.tile([P, CHUNKS, PASSES * CHUNK], U32, align_bytes=64)
+        w_scales = keep.tile([P, CHUNKS, PASSES * CHUNK], U8, align_bytes=64)
+
+        sum_sq = keep.tile([P, TILES], F32)
+        mean_sq = keep.tile([P, TILES], F32)
+        rms = keep.tile([P, TILES], F32)
+        inv_rms = keep.tile([P, TILES], F32)
+
+        def inverse_rms(a):
+            tiles = slice(PAIR * a, PAIR * (a + 1))
+            for t in range(PAIR * a, PAIR * (a + 1)):
+                squares = work.tile([P, DIM], BF16)
+                nc.scalar.activation(
+                    out=squares[:], in_=x_sb[:, t, :], func=ACT.Square, accum_out=sum_sq[:, t : t + 1]
+                )
+            nc.vector.tensor_scalar(
+                out=mean_sq[:, tiles],
+                in0=sum_sq[:, tiles],
+                scalar1=1.0 / DIM,
+                scalar2=RMS_EPS * RMS_EPS / DIM,
+                op0=ALU.mult,
+                op1=ALU.max,
+            )
+            nc.scalar.sqrt(rms[:, tiles], mean_sq[:, tiles])
+            nc.vector.reciprocal(inv_rms[:, tiles], rms[:, tiles])
+
+        def quantise_x(a):
+            x_grouped = work.tile([P, PAIR, DIM], BF16, align_bytes=64)
+            for i in range(PAIR):
+                t = PAIR * a + i
+                normed = work.tile([P, DIM], BF16)
+                nc.vector.scalar_tensor_tensor(
+                    out=normed[:],
+                    in0=x_sb[:, t, :],
+                    scalar=inv_rms[:, t : t + 1],
+                    in1=gamma_b[:],
+                    op0=ALU.mult,
+                    op1=ALU.mult,
+                )
+                normed_words = normed[:].bitcast(F32).rearrange(
+                    "m (g p u) -> m g u p", g=PASSES, u=HALF_PACK
+                )
+                turned = psum_turn.tile([P, PASSES, HALF_PACK, P], F32)
+                for g in range(PASSES):
+                    for u in range(HALF_PACK):
+                        nc.tensor.transpose(turned[:, g, u, :], normed_words[:, g, u, :], ident[:])
+                nc.scalar.copy(
+                    out=x_grouped[:, i, :].bitcast(F32).rearrange(
+                        "p (g m u) -> p g m u", g=PASSES, u=HALF_PACK
+                    ),
+                    in_=turned[:].rearrange("p g u m -> p g m u"),
+                )
+            tiles = slice(PAIR * a, PAIR * (a + 1))
+            nc.vector.quantize_mx(
+                out=x_codes[:, tiles, :].rearrange("p t w -> p (t w)").bitcast(FP8X4),
+                scales=x_scales[:, tiles, :].rearrange("p t w -> p (t w)"),
+                in_=x_grouped[:].rearrange("p t k -> p (t k)"),
+            )
+
+        def prepare_w(c):
+            w_raw_q = w_raw[c // CHUNKS_PER_TENSOR]
+            lo = (c % CHUNKS_PER_TENSOR) * CHUNK
+            w_grouped = work.tile([P, PASSES, CHUNK, PACK], BF16, align_bytes=64)
+            for g in range(PASSES):
+                nc.vector.tensor_copy(
+                    out=w_grouped[:, g, :, :].rearrange("p (c i) j -> p c j i", i=4),
+                    in_=w_raw_q[:, g, :, lo : lo + CHUNK].rearrange("p j (c i) -> p c j i", i=4),
+                )
+            nc.vector.quantize_mx(
+                out=w_codes[:, c, :].bitcast(FP8X4),
+                scales=w_scales[:, c, :],
+                in_=w_grouped[:].rearrange("p g n j -> p (g n j)"),
+            )
+
+        def project(c, a, stage):
+            acc = psum_acc.tile([P, PAIR, CHUNK], F32, tag="acc")
+            for i in range(PAIR):
+                t = PAIR * a + i
+                for g in range(PASSES):
+                    nc.tensor.matmul_mx(
+                        out=acc[:, i, :],
+                        lhsT=x_codes[:, t, g * P : (g + 1) * P].bitcast(FP8X4),
+                        lhsT_scale=x_scales[:, t, g * P : (g + 1) * P],
+                        rhs=w_codes[:, c, g * CHUNK : (g + 1) * CHUNK].bitcast(FP8X4),
+                        rhs_scale=w_scales[:, c, g * CHUNK : (g + 1) * CHUNK],
+                        start=(g == 0),
+                        stop=(g == PASSES - 1),
+                    )
+            dst = stage[:, :, PAIR * a : PAIR * (a + 1), :]
+            src = acc[:].rearrange("p i (h d) -> p h i d", h=CHUNK_HEADS)
+            is_q = c < CHUNKS_PER_TENSOR
+            if (c * PAIRS + a) % VECTOR_EVERY == VECTOR_EVERY - 1:
+                if is_q:
+                    nc.vector.tensor_scalar(
+                        out=dst, in0=src, scalar1=HEAD_DIM**-0.5, scalar2=None, op0=ALU.mult
+                    )
+                else:
+                    nc.vector.tensor_copy(out=dst, in_=src)
+            else:
+                if is_q:
+                    nc.scalar.mul(dst, src, HEAD_DIM**-0.5)
+                else:
+                    nc.scalar.copy(out=dst, in_=src)
+
+        def store(c, stage):
+            h0 = (c % CHUNKS_PER_TENSOR) * CHUNK_HEADS
+            nc.sync.dma_start(
+                out=out_views[c // CHUNKS_PER_TENSOR][:, h0 : h0 + CHUNK_HEADS, :],
+                in_=stage[:].rearrange("p h t d -> p h (t d)"),
+            )
+
+        stage = stages.tile([P, CHUNK_HEADS, TILES, HEAD_DIM], F32)
+        inverse_rms(0)
+        for a in range(PAIRS):
+            if a + 1 < PAIRS:
+                inverse_rms(a + 1)
+            quantise_x(a)
+            if a == 0:
+                prepare_w(0)
+            project(0, a, stage)
+        store(0, stage)
+
+        prepare_w(1)
+        for c in range(1, CHUNKS):
+            if c + 1 < CHUNKS:
+                prepare_w(c + 1)
+            stage = stages.tile([P, CHUNK_HEADS, TILES, HEAD_DIM], F32)
+            for a in range(PAIRS):
+                project(c, a, stage)
+            store(c, stage)

@@ -32,6 +32,11 @@ CHUNKS_PER_TENSOR = TENSOR_COLS // CHUNK
 CHUNKS = TENSORS * CHUNKS_PER_TENSOR
 BANK = 512
 VECTOR_EVERY = 8
+RMS_AHEAD = 3
+NORM_AHEAD = 2
+W_AHEAD = 2
+SQRT_FLOOR = 2.0**-112
+PSUM_BANKS = 8
 
 FLOPS = 2 * TOKENS * DIM * TENSORS * TENSOR_COLS
 
@@ -48,8 +53,7 @@ def tile_ringattention_pa_kernel(tc, x, gamma, w_qkv, out_0, out_1, out_2):
         keep = ctx.enter_context(tc.tile_pool(name="keep", bufs=1))
         work = ctx.enter_context(tc.tile_pool(name="work", bufs=3))
         stages = ctx.enter_context(tc.tile_pool(name="stages", bufs=4))
-        psum_turn = ctx.enter_context(tc.psum_pool(name="psum_turn", bufs=2))
-        psum_acc = ctx.enter_context(tc.psum_pool(name="psum_acc", bufs=6))
+        psum = ctx.enter_context(tc.psum_pool(name="psum", bufs=PSUM_BANKS))
 
         gamma_in = const.tile([1, DIM], BF16)
         nc.sync.dma_start(out=gamma_in[:], in_=gamma.rearrange("(o k) -> o k", o=1))
@@ -73,10 +77,10 @@ def tile_ringattention_pa_kernel(tc, x, gamma, w_qkv, out_0, out_1, out_2):
         make_identity(nc, ident[:])
         ones = const.tile([P, P], BF16)
         nc.vector.memset(ones[:], 1.0)
-        one_col = const.tile([P, 1], F32)
-        nc.vector.memset(one_col[:], 1.0)
+        sqrt_floor = const.tile([P, 1], F32)
+        nc.vector.memset(sqrt_floor[:], SQRT_FLOOR)
         sqrt_warm = const.tile([P, 1], F32)
-        nc.scalar.sqrt(sqrt_warm[:], one_col[:])
+        nc.scalar.sqrt(sqrt_warm[:], sqrt_floor[:])
 
         gamma_row = const.tile([P, DIM], BF16)
         nc.vector.memset(gamma_row[:], 0.0)
@@ -84,7 +88,7 @@ def tile_ringattention_pa_kernel(tc, x, gamma, w_qkv, out_0, out_1, out_2):
         gamma_b = const.tile([P, DIM], BF16)
         for half in range(DIM // BANK):
             cols = slice(half * BANK, (half + 1) * BANK)
-            spread = psum_acc.tile([P, BANK], F32, tag="acc")
+            spread = psum.tile([P, BANK], F32, tag="bank")
             nc.tensor.matmul(out=spread[:], lhsT=ones[:], rhs=gamma_row[:, cols], start=True, stop=True)
             nc.vector.tensor_copy(out=gamma_b[:, cols], in_=spread[:])
 
@@ -94,32 +98,28 @@ def tile_ringattention_pa_kernel(tc, x, gamma, w_qkv, out_0, out_1, out_2):
         w_scales = keep.tile([P, CHUNKS, PASSES * CHUNK], U8, align_bytes=64)
 
         sum_sq = keep.tile([P, TILES], F32)
-        mean_sq = keep.tile([P, TILES], F32)
         rms = keep.tile([P, TILES], F32)
+        rms_clamped = keep.tile([P, TILES], F32)
         inv_rms = keep.tile([P, TILES], F32)
+        turned = {}
+        x_grouped = {}
 
-        def inverse_rms(a):
+        def root_mean_square(a):
             tiles = slice(PAIR * a, PAIR * (a + 1))
             for t in range(PAIR * a, PAIR * (a + 1)):
                 squares = work.tile([P, DIM], BF16)
                 nc.scalar.activation(
                     out=squares[:], in_=x_sb[:, t, :], func=ACT.Square, accum_out=sum_sq[:, t : t + 1]
                 )
-            nc.vector.tensor_scalar(
-                out=mean_sq[:, tiles],
-                in0=sum_sq[:, tiles],
-                scalar1=1.0 / DIM,
-                scalar2=RMS_EPS * RMS_EPS / DIM,
-                op0=ALU.mult,
-                op1=ALU.max,
+            nc.scalar.activation(
+                out=rms[:, tiles], in_=sum_sq[:, tiles], func=ACT.Sqrt, scale=1.0 / DIM, bias=sqrt_floor[:]
             )
-            nc.scalar.sqrt(rms[:, tiles], mean_sq[:, tiles])
-            nc.vector.reciprocal(inv_rms[:, tiles], rms[:, tiles])
 
-        def quantise_x(a):
-            x_grouped = work.tile([P, PAIR, DIM], BF16, align_bytes=64)
-            for i in range(PAIR):
-                t = PAIR * a + i
+        def normalise(a):
+            tiles = slice(PAIR * a, PAIR * (a + 1))
+            nc.vector.tensor_scalar_max(out=rms_clamped[:, tiles], in0=rms[:, tiles], scalar1=RMS_EPS / DIM**0.5)
+            nc.vector.reciprocal(inv_rms[:, tiles], rms_clamped[:, tiles])
+            for t in range(PAIR * a, PAIR * (a + 1)):
                 normed = work.tile([P, DIM], BF16)
                 nc.vector.scalar_tensor_tensor(
                     out=normed[:],
@@ -132,21 +132,27 @@ def tile_ringattention_pa_kernel(tc, x, gamma, w_qkv, out_0, out_1, out_2):
                 normed_words = normed[:].bitcast(F32).rearrange(
                     "m (g p u) -> m g u p", g=PASSES, u=HALF_PACK
                 )
-                turned = psum_turn.tile([P, PASSES, HALF_PACK, P], F32)
+                turned[t] = psum.tile([P, PASSES, HALF_PACK, P], F32, name="turned", tag="bank")
                 for g in range(PASSES):
                     for u in range(HALF_PACK):
-                        nc.tensor.transpose(turned[:, g, u, :], normed_words[:, g, u, :], ident[:])
+                        nc.tensor.transpose(turned[t][:, g, u, :], normed_words[:, g, u, :], ident[:])
+
+        def regroup_x(a):
+            x_grouped[a] = work.tile([P, PAIR, DIM], BF16, name="x_grouped", align_bytes=64)
+            for i in range(PAIR):
                 nc.scalar.copy(
-                    out=x_grouped[:, i, :].bitcast(F32).rearrange(
+                    out=x_grouped[a][:, i, :].bitcast(F32).rearrange(
                         "p (g m u) -> p g m u", g=PASSES, u=HALF_PACK
                     ),
-                    in_=turned[:].rearrange("p g u m -> p g m u"),
+                    in_=turned[PAIR * a + i][:].rearrange("p g u m -> p g m u"),
                 )
+
+        def quantise_x(a):
             tiles = slice(PAIR * a, PAIR * (a + 1))
             nc.vector.quantize_mx(
                 out=x_codes[:, tiles, :].rearrange("p t w -> p (t w)").bitcast(FP8X4),
                 scales=x_scales[:, tiles, :].rearrange("p t w -> p (t w)"),
-                in_=x_grouped[:].rearrange("p t k -> p (t k)"),
+                in_=x_grouped[a][:].rearrange("p t k -> p (t k)"),
             )
 
         def prepare_w(c):
@@ -164,13 +170,15 @@ def tile_ringattention_pa_kernel(tc, x, gamma, w_qkv, out_0, out_1, out_2):
                 in_=w_grouped[:].rearrange("p g n j -> p (g n j)"),
             )
 
-        def project(c, a, stage):
-            acc = psum_acc.tile([P, PAIR, CHUNK], F32, tag="acc")
+        acc = {}
+
+        def project(c, a):
+            acc[c, a] = psum.tile([P, PAIR, CHUNK], F32, name="acc", tag="bank")
             for i in range(PAIR):
                 t = PAIR * a + i
                 for g in range(PASSES):
                     nc.tensor.matmul_mx(
-                        out=acc[:, i, :],
+                        out=acc[c, a][:, i, :],
                         lhsT=x_codes[:, t, g * P : (g + 1) * P].bitcast(FP8X4),
                         lhsT_scale=x_scales[:, t, g * P : (g + 1) * P],
                         rhs=w_codes[:, c, g * CHUNK : (g + 1) * CHUNK].bitcast(FP8X4),
@@ -178,8 +186,10 @@ def tile_ringattention_pa_kernel(tc, x, gamma, w_qkv, out_0, out_1, out_2):
                         start=(g == 0),
                         stop=(g == PASSES - 1),
                     )
+
+        def evacuate(c, a, stage):
             dst = stage[:, :, PAIR * a : PAIR * (a + 1), :]
-            src = acc[:].rearrange("p i (h d) -> p h i d", h=CHUNK_HEADS)
+            src = acc[c, a][:].rearrange("p i (h d) -> p h i d", h=CHUNK_HEADS)
             is_q = c < CHUNKS_PER_TENSOR
             if (c * PAIRS + a) % VECTOR_EVERY == VECTOR_EVERY - 1:
                 if is_q:
@@ -201,22 +211,32 @@ def tile_ringattention_pa_kernel(tc, x, gamma, w_qkv, out_0, out_1, out_2):
                 in_=stage[:].rearrange("p h t d -> p h (t d)"),
             )
 
+        for a in range(RMS_AHEAD):
+            root_mean_square(a)
+        for a in range(NORM_AHEAD):
+            normalise(a)
+        prepare_w(0)
         stage = stages.tile([P, CHUNK_HEADS, TILES, HEAD_DIM], F32)
-        inverse_rms(0)
         for a in range(PAIRS):
-            if a + 1 < PAIRS:
-                inverse_rms(a + 1)
+            regroup_x(a)
+            if a + RMS_AHEAD < PAIRS:
+                root_mean_square(a + RMS_AHEAD)
+            if a > 0:
+                evacuate(0, a - 1, stage)
             quantise_x(a)
-            if a == 0:
-                prepare_w(0)
-            project(0, a, stage)
+            project(0, a)
+            if a + NORM_AHEAD < PAIRS:
+                normalise(a + NORM_AHEAD)
+        evacuate(0, PAIRS - 1, stage)
         store(0, stage)
 
-        prepare_w(1)
+        for c in range(1, 1 + W_AHEAD):
+            prepare_w(c)
         for c in range(1, CHUNKS):
-            if c + 1 < CHUNKS:
-                prepare_w(c + 1)
+            if c + W_AHEAD < CHUNKS:
+                prepare_w(c + W_AHEAD)
             stage = stages.tile([P, CHUNK_HEADS, TILES, HEAD_DIM], F32)
             for a in range(PAIRS):
-                project(c, a, stage)
+                project(c, a)
+                evacuate(c, a, stage)
             store(c, stage)

@@ -34,7 +34,8 @@ BANK = 512
 VECTOR_EVERY = 8
 RMS_AHEAD = 3
 NORM_AHEAD = 2
-W_AHEAD = 2
+EARLY_CHUNKS = 2
+LATE_CHUNKS = 2
 SQRT_FLOOR = 2.0**-112
 PSUM_BANKS = 8
 
@@ -45,7 +46,7 @@ def tile_ringattention_pa_kernel(tc, x, gamma, w_qkv, out_0, out_1, out_2):
     nc = tc.nc
 
     x_view = x.rearrange("b (p t) k -> p (b t) k", t=TILES)
-    out_views = [o.rearrange("b h (p t) d -> p (b h) (t d)", t=TILES) for o in (out_0, out_1, out_2)]
+    out_views = [o.rearrange("b h (p t) d -> p (b h) t d", t=TILES) for o in (out_0, out_1, out_2)]
     w_view = w_qkv.rearrange("(g p j) n -> g p j n", g=PASSES, j=PACK)
 
     with ExitStack() as ctx:
@@ -54,24 +55,36 @@ def tile_ringattention_pa_kernel(tc, x, gamma, w_qkv, out_0, out_1, out_2):
         work = ctx.enter_context(tc.tile_pool(name="work", bufs=3))
         stages = ctx.enter_context(tc.tile_pool(name="stages", bufs=4))
         psum = ctx.enter_context(tc.psum_pool(name="psum", bufs=PSUM_BANKS))
+        ctx.enter_context(tc.manual_schedule())
 
         gamma_in = const.tile([1, DIM], BF16)
         nc.sync.dma_start(out=gamma_in[:], in_=gamma.rearrange("(o k) -> o k", o=1))
 
         x_sb = keep.tile([P, TILES, DIM], BF16)
-        for a in range(PAIRS):
+
+        def load_x(a):
             tiles = slice(PAIR * a, PAIR * (a + 1))
             nc.sync.dma_start(out=x_sb[:, tiles, :], in_=x_view[:, tiles, :])
 
-        w_raw = []
-        for q in range(TENSORS):
-            w_raw_q = keep.tile([P, PASSES, PACK, TENSOR_COLS], BF16, name="w_raw%d" % q)
+        w_raw = {}
+
+        def load_w(first, chunks):
+            cols = chunks * CHUNK
+            raw = keep.tile([P, PASSES, PACK, cols], BF16, name="w_raw%d" % first)
             for g in range(PASSES):
                 nc.sync.dma_start(
-                    out=w_raw_q[:, g, :, :],
-                    in_=w_view[g, :, :, q * TENSOR_COLS : (q + 1) * TENSOR_COLS],
+                    out=raw[:, g, :, :], in_=w_view[g, :, :, first * CHUNK : first * CHUNK + cols]
                 )
-            w_raw.append(w_raw_q)
+            for c in range(chunks):
+                w_raw[first + c] = (raw, c * CHUNK)
+
+        load_x(0)
+        load_w(0, 1)
+        for a in range(1, PAIRS):
+            load_x(a)
+        load_w(1, CHUNKS_PER_TENSOR - 1)
+        for q in range(1, TENSORS):
+            load_w(q * CHUNKS_PER_TENSOR, CHUNKS_PER_TENSOR)
 
         ident = const.tile([P, P], F32)
         make_identity(nc, ident[:])
@@ -155,19 +168,22 @@ def tile_ringattention_pa_kernel(tc, x, gamma, w_qkv, out_0, out_1, out_2):
                 in_=x_grouped[a][:].rearrange("p t k -> p (t k)"),
             )
 
-        def prepare_w(c):
-            w_raw_q = w_raw[c // CHUNKS_PER_TENSOR]
-            lo = (c % CHUNKS_PER_TENSOR) * CHUNK
-            w_grouped = work.tile([P, PASSES, CHUNK, PACK], BF16, align_bytes=64)
+        w_grouped = {}
+
+        def regroup_w(c):
+            raw, lo = w_raw[c]
+            w_grouped[c] = work.tile([P, PASSES, CHUNK, PACK], BF16, name="w_grouped", align_bytes=64)
             for g in range(PASSES):
                 nc.vector.tensor_copy(
-                    out=w_grouped[:, g, :, :].rearrange("p (c i) j -> p c j i", i=4),
-                    in_=w_raw_q[:, g, :, lo : lo + CHUNK].rearrange("p j (c i) -> p c j i", i=4),
+                    out=w_grouped[c][:, g, :, :].rearrange("p (c i) j -> p c j i", i=4),
+                    in_=raw[:, g, :, lo : lo + CHUNK].rearrange("p j (c i) -> p c j i", i=4),
                 )
+
+        def quantise_w(c):
             nc.vector.quantize_mx(
                 out=w_codes[:, c, :].bitcast(FP8X4),
                 scales=w_scales[:, c, :],
-                in_=w_grouped[:].rearrange("p g n j -> p (g n j)"),
+                in_=w_grouped[c][:].rearrange("p g n j -> p (g n j)"),
             )
 
         acc = {}
@@ -187,8 +203,12 @@ def tile_ringattention_pa_kernel(tc, x, gamma, w_qkv, out_0, out_1, out_2):
                         stop=(g == PASSES - 1),
                     )
 
-        def evacuate(c, a, stage):
-            dst = stage[:, :, PAIR * a : PAIR * (a + 1), :]
+        stage = {}
+
+        def evacuate(c, a):
+            if a == 0:
+                stage[c] = stages.tile([P, CHUNK_HEADS, TILES, HEAD_DIM], F32, name="stage")
+            dst = stage[c][:, :, PAIR * a : PAIR * (a + 1), :]
             src = acc[c, a][:].rearrange("p i (h d) -> p h i d", h=CHUNK_HEADS)
             is_q = c < CHUNKS_PER_TENSOR
             if (c * PAIRS + a) % VECTOR_EVERY == VECTOR_EVERY - 1:
@@ -203,40 +223,56 @@ def tile_ringattention_pa_kernel(tc, x, gamma, w_qkv, out_0, out_1, out_2):
                     nc.scalar.mul(dst, src, HEAD_DIM**-0.5)
                 else:
                     nc.scalar.copy(out=dst, in_=src)
+            in_halves = c < EARLY_CHUNKS or c >= CHUNKS - LATE_CHUNKS
+            pairs_per_store = PAIRS // 2 if in_halves else PAIRS
+            if (a + 1) % pairs_per_store == 0:
+                tiles = slice(PAIR * (a + 1 - pairs_per_store), PAIR * (a + 1))
+                h0 = (c % CHUNKS_PER_TENSOR) * CHUNK_HEADS
+                nc.sync.dma_start(
+                    out=out_views[c // CHUNKS_PER_TENSOR][:, h0 : h0 + CHUNK_HEADS, tiles, :],
+                    in_=stage[c][:, :, tiles, :],
+                )
 
-        def store(c, stage):
-            h0 = (c % CHUNKS_PER_TENSOR) * CHUNK_HEADS
-            nc.sync.dma_start(
-                out=out_views[c // CHUNKS_PER_TENSOR][:, h0 : h0 + CHUNK_HEADS, :],
-                in_=stage[:].rearrange("p h t d -> p h (t d)"),
-            )
+        def early_banks(a):
+            banks = [(0, a)]
+            if a == PAIRS - 2:
+                banks.extend([(1, b) for b in range(a + 1)])
+            if a == PAIRS - 1:
+                banks.append((1, a))
+            return banks
 
+        regroup_w(0)
+        quantise_w(0)
         for a in range(RMS_AHEAD):
             root_mean_square(a)
         for a in range(NORM_AHEAD):
             normalise(a)
-        prepare_w(0)
-        stage = stages.tile([P, CHUNK_HEADS, TILES, HEAD_DIM], F32)
+        regroup_w(1)
         for a in range(PAIRS):
             regroup_x(a)
             if a + RMS_AHEAD < PAIRS:
                 root_mean_square(a + RMS_AHEAD)
             if a > 0:
-                evacuate(0, a - 1, stage)
+                for c, b in early_banks(a - 1):
+                    evacuate(c, b)
             quantise_x(a)
-            project(0, a)
+            if a == PAIRS - 2:
+                quantise_w(1)
+                regroup_w(2)
+            for c, b in early_banks(a):
+                project(c, b)
             if a + NORM_AHEAD < PAIRS:
                 normalise(a + NORM_AHEAD)
-        evacuate(0, PAIRS - 1, stage)
-        store(0, stage)
+        quantise_w(2)
+        regroup_w(3)
+        for c, b in early_banks(PAIRS - 1):
+            evacuate(c, b)
 
-        for c in range(1, 1 + W_AHEAD):
-            prepare_w(c)
-        for c in range(1, CHUNKS):
-            if c + W_AHEAD < CHUNKS:
-                prepare_w(c + W_AHEAD)
-            stage = stages.tile([P, CHUNK_HEADS, TILES, HEAD_DIM], F32)
+        for c in range(EARLY_CHUNKS, CHUNKS):
+            if c + 1 < CHUNKS:
+                quantise_w(c + 1)
+            if c + 2 < CHUNKS:
+                regroup_w(c + 2)
             for a in range(PAIRS):
                 project(c, a)
-                evacuate(c, a, stage)
-            store(c, stage)
+                evacuate(c, a)

@@ -36,7 +36,8 @@ RMS_AHEAD = 3
 NORM_AHEAD = 2
 EARLY_CHUNKS = 2
 LATE_CHUNKS = 2
-SQRT_FLOOR = 2.0**-112
+ROOT_DIM = 32.0
+assert ROOT_DIM * ROOT_DIM == DIM
 PSUM_BANKS = 8
 
 FLOPS = 2 * TOKENS * DIM * TENSORS * TENSOR_COLS
@@ -54,7 +55,8 @@ def tile_ringattention_pa_kernel(tc, x, gamma, w_qkv, out_0, out_1, out_2):
         keep = ctx.enter_context(tc.tile_pool(name="keep", bufs=1))
         work = ctx.enter_context(tc.tile_pool(name="work", bufs=3))
         stages = ctx.enter_context(tc.tile_pool(name="stages", bufs=4))
-        psum = ctx.enter_context(tc.psum_pool(name="psum", bufs=PSUM_BANKS))
+        psum_gamma = ctx.enter_context(tc.psum_pool(name="psum_gamma", bufs=1))
+        psum = ctx.enter_context(tc.psum_pool(name="psum", bufs=PSUM_BANKS - 1))
         ctx.enter_context(tc.manual_schedule())
 
         gamma_in = const.tile([1, DIM], BF16)
@@ -88,22 +90,22 @@ def tile_ringattention_pa_kernel(tc, x, gamma, w_qkv, out_0, out_1, out_2):
 
         ident = const.tile([P, P], F32)
         make_identity(nc, ident[:])
-        ones = const.tile([P, P], BF16)
-        nc.vector.memset(ones[:], 1.0)
-        sqrt_floor = const.tile([P, 1], F32)
-        nc.vector.memset(sqrt_floor[:], SQRT_FLOOR)
-        sqrt_warm = const.tile([P, 1], F32)
-        nc.scalar.sqrt(sqrt_warm[:], sqrt_floor[:])
+        spreader = const.tile([P, P], BF16)
+        nc.vector.memset(spreader[:], ROOT_DIM)
+        minus_half = const.tile([P, TILES], F32)
+        nc.vector.memset(minus_half[:], -0.5)
+        warm = const.tile([P, 1], F32)
+        nc.scalar.square(warm[:], minus_half[:, 0:1])
 
         gamma_row = const.tile([P, DIM], BF16)
         nc.vector.memset(gamma_row[:], 0.0)
         nc.vector.tensor_copy(out=gamma_row[0:1, :], in_=gamma_in[:])
-        gamma_b = const.tile([P, DIM], BF16)
+        gamma_b = psum_gamma.tile([P, DIM], BF16)
         for half in range(DIM // BANK):
             cols = slice(half * BANK, (half + 1) * BANK)
-            spread = psum.tile([P, BANK], F32, tag="bank")
-            nc.tensor.matmul(out=spread[:], lhsT=ones[:], rhs=gamma_row[:, cols], start=True, stop=True)
-            nc.vector.tensor_copy(out=gamma_b[:, cols], in_=spread[:])
+            nc.tensor.matmul(
+                out=gamma_b[:, cols], lhsT=spreader[:], rhs=gamma_row[:, cols], start=True, stop=True
+            )
 
         x_codes = keep.tile([P, TILES, PASSES * P], U32, align_bytes=64)
         x_scales = keep.tile([P, TILES, PASSES * P], U8, align_bytes=64)
@@ -111,33 +113,30 @@ def tile_ringattention_pa_kernel(tc, x, gamma, w_qkv, out_0, out_1, out_2):
         w_scales = keep.tile([P, CHUNKS, PASSES * CHUNK], U8, align_bytes=64)
 
         sum_sq = keep.tile([P, TILES], F32)
-        rms = keep.tile([P, TILES], F32)
-        rms_clamped = keep.tile([P, TILES], F32)
-        inv_rms = keep.tile([P, TILES], F32)
+        sum_sq_clamped = keep.tile([P, TILES], F32)
+        inv_l2 = keep.tile([P, TILES], F32)
         turned = {}
         x_grouped = {}
 
-        def root_mean_square(a):
+        def inverse_norm(a):
             tiles = slice(PAIR * a, PAIR * (a + 1))
             for t in range(PAIR * a, PAIR * (a + 1)):
                 squares = work.tile([P, DIM], BF16)
                 nc.scalar.activation(
                     out=squares[:], in_=x_sb[:, t, :], func=ACT.Square, accum_out=sum_sq[:, t : t + 1]
                 )
-            nc.scalar.activation(
-                out=rms[:, tiles], in_=sum_sq[:, tiles], func=ACT.Sqrt, scale=1.0 / DIM, bias=sqrt_floor[:]
+            nc.gpsimd.tensor_scalar_max(out=sum_sq_clamped[:, tiles], in0=sum_sq[:, tiles], scalar1=RMS_EPS * RMS_EPS)
+            nc.gpsimd.tensor_tensor(
+                out=inv_l2[:, tiles], in0=sum_sq_clamped[:, tiles], in1=minus_half[:, tiles], op=ALU.pow
             )
 
         def normalise(a):
-            tiles = slice(PAIR * a, PAIR * (a + 1))
-            nc.vector.tensor_scalar_max(out=rms_clamped[:, tiles], in0=rms[:, tiles], scalar1=RMS_EPS / DIM**0.5)
-            nc.vector.reciprocal(inv_rms[:, tiles], rms_clamped[:, tiles])
             for t in range(PAIR * a, PAIR * (a + 1)):
                 normed = work.tile([P, DIM], BF16)
                 nc.vector.scalar_tensor_tensor(
                     out=normed[:],
                     in0=x_sb[:, t, :],
-                    scalar=inv_rms[:, t : t + 1],
+                    scalar=inv_l2[:, t : t + 1],
                     in1=gamma_b[:],
                     op0=ALU.mult,
                     op1=ALU.mult,
@@ -244,14 +243,14 @@ def tile_ringattention_pa_kernel(tc, x, gamma, w_qkv, out_0, out_1, out_2):
         regroup_w(0)
         quantise_w(0)
         for a in range(RMS_AHEAD):
-            root_mean_square(a)
+            inverse_norm(a)
         for a in range(NORM_AHEAD):
             normalise(a)
         regroup_w(1)
         for a in range(PAIRS):
             regroup_x(a)
             if a + RMS_AHEAD < PAIRS:
-                root_mean_square(a + RMS_AHEAD)
+                inverse_norm(a + RMS_AHEAD)
             if a > 0:
                 for c, b in early_banks(a - 1):
                     evacuate(c, b)

@@ -82,9 +82,11 @@ def tile_ringattention_pa_kernel(tc, x, gamma, w_qkv, out_0, out_1, out_2):
 
         load_x(0)
         load_w(0, 1)
-        for a in range(1, PAIRS):
+        load_x(1)
+        load_w(1, 1)
+        for a in range(2, PAIRS):
             load_x(a)
-        load_w(1, CHUNKS_PER_TENSOR - 1)
+        load_w(2, CHUNKS_PER_TENSOR - 2)
         for q in range(1, TENSORS):
             load_w(q * CHUNKS_PER_TENSOR, CHUNKS_PER_TENSOR)
 
@@ -178,6 +180,19 @@ def tile_ringattention_pa_kernel(tc, x, gamma, w_qkv, out_0, out_1, out_2):
                     in_=raw[:, g, :, lo : lo + CHUNK].rearrange("p j (c i) -> p c j i", i=4),
                 )
 
+        def regroup_w_on_gpsimd(c, g):
+            raw, lo = w_raw[c]
+            if g == 0:
+                w_grouped[c] = work.tile([P, PASSES, CHUNK, PACK], BF16, name="w_grouped", align_bytes=64)
+            nc.gpsimd.tensor_scalar(
+                out=w_grouped[c][:, g, :, :],
+                in0=raw[:, g, :, lo : lo + CHUNK].rearrange("p j n -> p n j"),
+                scalar1=1.0,
+                scalar2=0.0,
+                op0=ALU.mult,
+                op1=ALU.add,
+            )
+
         def quantise_w(c):
             nc.vector.quantize_mx(
                 out=w_codes[:, c, :].bitcast(FP8X4),
@@ -232,39 +247,35 @@ def tile_ringattention_pa_kernel(tc, x, gamma, w_qkv, out_0, out_1, out_2):
                     in_=stage[c][:, :, tiles, :],
                 )
 
-        def early_banks(a):
-            banks = [(0, a)]
-            if a == PAIRS - 2:
-                banks.extend([(1, b) for b in range(a + 1)])
-            if a == PAIRS - 1:
-                banks.append((1, a))
-            return banks
-
         regroup_w(0)
         quantise_w(0)
         for a in range(RMS_AHEAD):
             inverse_norm(a)
+            if a < PASSES:
+                regroup_w_on_gpsimd(1, a)
         for a in range(NORM_AHEAD):
             normalise(a)
-        regroup_w(1)
+        filled = []
         for a in range(PAIRS):
             regroup_x(a)
             if a + RMS_AHEAD < PAIRS:
                 inverse_norm(a + RMS_AHEAD)
-            if a > 0:
-                for c, b in early_banks(a - 1):
-                    evacuate(c, b)
+            for c, b in filled[:a]:
+                evacuate(c, b)
+            filled = filled[a:]
             quantise_x(a)
-            if a == PAIRS - 2:
+            if a == 0:
                 quantise_w(1)
+            if a == PAIRS - 2:
                 regroup_w(2)
-            for c, b in early_banks(a):
-                project(c, b)
+            for c in range(EARLY_CHUNKS):
+                project(c, a)
+                filled.append((c, a))
             if a + NORM_AHEAD < PAIRS:
                 normalise(a + NORM_AHEAD)
         quantise_w(2)
         regroup_w(3)
-        for c, b in early_banks(PAIRS - 1):
+        for c, b in filled:
             evacuate(c, b)
 
         for c in range(EARLY_CHUNKS, CHUNKS):

@@ -121,16 +121,17 @@ def tile_ringattention_pa_kernel(tc, x, gamma, w_qkv, out_0, out_1, out_2):
         x_grouped = {}
 
         def inverse_norm(a):
-            tiles = slice(PAIR * a, PAIR * (a + 1))
             for t in range(PAIR * a, PAIR * (a + 1)):
                 squares = work.tile([P, DIM], BF16)
                 nc.scalar.activation(
                     out=squares[:], in_=x_sb[:, t, :], func=ACT.Square, accum_out=sum_sq[:, t : t + 1]
                 )
-            nc.gpsimd.tensor_scalar_max(out=sum_sq_clamped[:, tiles], in0=sum_sq[:, tiles], scalar1=RMS_EPS * RMS_EPS)
-            nc.gpsimd.tensor_tensor(
-                out=inv_l2[:, tiles], in0=sum_sq_clamped[:, tiles], in1=minus_half[:, tiles], op=ALU.pow
-            )
+                nc.gpsimd.tensor_scalar_max(
+                    out=sum_sq_clamped[:, t : t + 1], in0=sum_sq[:, t : t + 1], scalar1=RMS_EPS * RMS_EPS
+                )
+                nc.gpsimd.tensor_tensor(
+                    out=inv_l2[:, t : t + 1], in0=sum_sq_clamped[:, t : t + 1], in1=minus_half[:, t : t + 1], op=ALU.pow
+                )
 
         def normalise(a):
             for t in range(PAIR * a, PAIR * (a + 1)):
@@ -171,26 +172,20 @@ def tile_ringattention_pa_kernel(tc, x, gamma, w_qkv, out_0, out_1, out_2):
 
         w_grouped = {}
 
-        def regroup_w(c):
+        def regroup_w(c, passes=PASSES):
             raw, lo = w_raw[c]
             w_grouped[c] = work.tile([P, PASSES, CHUNK, PACK], BF16, name="w_grouped", align_bytes=64)
-            for g in range(PASSES):
+            for g in range(passes):
                 nc.vector.tensor_copy(
                     out=w_grouped[c][:, g, :, :].rearrange("p (c i) j -> p c j i", i=4),
                     in_=raw[:, g, :, lo : lo + CHUNK].rearrange("p j (c i) -> p c j i", i=4),
                 )
 
-        def regroup_w_on_gpsimd(c, g):
+        def regroup_w_on_scalar(c, g):
             raw, lo = w_raw[c]
-            if g == 0:
-                w_grouped[c] = work.tile([P, PASSES, CHUNK, PACK], BF16, name="w_grouped", align_bytes=64)
-            nc.gpsimd.tensor_scalar(
+            nc.scalar.copy(
                 out=w_grouped[c][:, g, :, :],
-                in0=raw[:, g, :, lo : lo + CHUNK].rearrange("p j n -> p n j"),
-                scalar1=1.0,
-                scalar2=0.0,
-                op0=ALU.mult,
-                op1=ALU.add,
+                in_=raw[:, g, :, lo : lo + CHUNK].rearrange("p j n -> p n j"),
             )
 
         def quantise_w(c):
@@ -251,10 +246,9 @@ def tile_ringattention_pa_kernel(tc, x, gamma, w_qkv, out_0, out_1, out_2):
         quantise_w(0)
         for a in range(RMS_AHEAD):
             inverse_norm(a)
-            if a < PASSES:
-                regroup_w_on_gpsimd(1, a)
         for a in range(NORM_AHEAD):
             normalise(a)
+        regroup_w(1)
         filled = []
         for a in range(PAIRS):
             regroup_x(a)

@@ -163,6 +163,14 @@ def tile_ringattention_pa_kernel(tc, x, gamma, w_qkv, out_0, out_1, out_2):
                 )
 
         def quantise_x(a):
+            if a == PAIRS - 1:
+                for i in range(PAIR):
+                    nc.vector.quantize_mx(
+                        out=x_codes[:, PAIR * a + i, :].bitcast(FP8X4),
+                        scales=x_scales[:, PAIR * a + i, :],
+                        in_=x_grouped[a][:, i, :],
+                    )
+                return
             tiles = slice(PAIR * a, PAIR * (a + 1))
             nc.vector.quantize_mx(
                 out=x_codes[:, tiles, :].rearrange("p t w -> p (t w)").bitcast(FP8X4),

@@ -87,8 +87,7 @@ def tile_ringattention_pa_kernel(tc, x, gamma, w_qkv, out_0, out_1, out_2):
         for a in range(2, PAIRS):
             load_x(a)
         load_w(2, CHUNKS_PER_TENSOR - 2)
-        for q in range(1, TENSORS):
-            load_w(q * CHUNKS_PER_TENSOR, CHUNKS_PER_TENSOR)
+        load_w(CHUNKS_PER_TENSOR, CHUNKS - CHUNKS_PER_TENSOR)
 
         ident = const.tile([P, P], F32)
         make_identity(nc, ident[:])

@@ -31,11 +31,11 @@ TENSOR_COLS = HEADS * HEAD_DIM
 CHUNKS_PER_TENSOR = TENSOR_COLS // CHUNK
 CHUNKS = TENSORS * CHUNKS_PER_TENSOR
 BANK = 512
-VECTOR_EVERY = 8
+VECTOR_EVERY = 16
 RMS_AHEAD = 3
 NORM_AHEAD = 2
 EARLY_CHUNKS = 2
-LATE_CHUNKS = 2
+HALVED_CHUNKS = 4
 ROOT_DIM = 32.0
 assert ROOT_DIM * ROOT_DIM == DIM
 PSUM_BANKS = 8
@@ -82,9 +82,10 @@ def tile_ringattention_pa_kernel(tc, x, gamma, w_qkv, out_0, out_1, out_2):
 
         load_x(0)
         load_w(0, 1)
-        load_x(1)
+        for a in range(1, RMS_AHEAD):
+            load_x(a)
         load_w(1, 1)
-        for a in range(2, PAIRS):
+        for a in range(RMS_AHEAD, PAIRS):
             load_x(a)
         load_w(2, CHUNKS_PER_TENSOR - 2)
         load_w(CHUNKS_PER_TENSOR, CHUNKS - CHUNKS_PER_TENSOR)
@@ -239,7 +240,7 @@ def tile_ringattention_pa_kernel(tc, x, gamma, w_qkv, out_0, out_1, out_2):
                     nc.scalar.mul(dst, src, HEAD_DIM**-0.5)
                 else:
                     nc.scalar.copy(out=dst, in_=src)
-            in_halves = c < EARLY_CHUNKS or c >= CHUNKS - LATE_CHUNKS
+            in_halves = c < HALVED_CHUNKS
             pairs_per_store = PAIRS // 2 if in_halves else PAIRS
             if (a + 1) % pairs_per_store == 0:
                 tiles = slice(PAIR * (a + 1 - pairs_per_store), PAIR * (a + 1))

@@ -221,6 +221,14 @@ def tile_ringattention_pa_kernel(tc, x, gamma, w_qkv, out_0, out_1, out_2):
                     )
 
         stage = {}
+        deferred = []
+
+        def store(engine, c, tiles):
+            h0 = (c % CHUNKS_PER_TENSOR) * CHUNK_HEADS
+            engine.dma_start(
+                out=out_views[c // CHUNKS_PER_TENSOR][:, h0 : h0 + CHUNK_HEADS, tiles, :],
+                in_=stage[c][:, :, tiles, :],
+            )
 
         def evacuate(c, a):
             if a == 0:
@@ -244,11 +252,14 @@ def tile_ringattention_pa_kernel(tc, x, gamma, w_qkv, out_0, out_1, out_2):
             pairs_per_store = PAIRS // 2 if in_halves else PAIRS
             if (a + 1) % pairs_per_store == 0:
                 tiles = slice(PAIR * (a + 1 - pairs_per_store), PAIR * (a + 1))
-                h0 = (c % CHUNKS_PER_TENSOR) * CHUNK_HEADS
-                nc.sync.dma_start(
-                    out=out_views[c // CHUNKS_PER_TENSOR][:, h0 : h0 + CHUNK_HEADS, tiles, :],
-                    in_=stage[c][:, :, tiles, :],
-                )
+                if c % 2 == 0 and not in_halves:
+                    deferred.append((c, tiles))
+                else:
+                    store(nc.sync, c, tiles)
+            if a == 0:
+                for d, tiles in deferred:
+                    store(nc.scalar, d, tiles)
+                deferred.clear()
 
         regroup_w(0)
         quantise_w(0)

@@ -60,7 +60,7 @@ def tile_ringattention_pa_kernel(tc, x, gamma, w_qkv, out_0, out_1, out_2):
         ctx.enter_context(tc.manual_schedule())
 
         gamma_in = const.tile([1, DIM], BF16)
-        nc.sync.dma_start(out=gamma_in[:], in_=gamma.rearrange("(o k) -> o k", o=1))
+        nc.scalar.dma_start(out=gamma_in[:], in_=gamma.rearrange("(o k) -> o k", o=1))
 
         x_sb = keep.tile([P, TILES, DIM], BF16)
 
@@ -84,11 +84,10 @@ def tile_ringattention_pa_kernel(tc, x, gamma, w_qkv, out_0, out_1, out_2):
         load_w(0, 1)
         for a in range(1, RMS_AHEAD):
             load_x(a)
-        load_w(1, 1)
+        load_w(1, 2)
         for a in range(RMS_AHEAD, PAIRS):
             load_x(a)
-        load_w(2, CHUNKS_PER_TENSOR - 2)
-        load_w(CHUNKS_PER_TENSOR, CHUNKS - CHUNKS_PER_TENSOR)
+        load_w(3, CHUNKS - 3)
 
         ident = const.tile([P, P], F32)
         make_identity(nc, ident[:])
@@ -98,6 +97,10 @@ def tile_ringattention_pa_kernel(tc, x, gamma, w_qkv, out_0, out_1, out_2):
         nc.vector.memset(minus_half[:], -0.5)
         warm = const.tile([P, 1], F32)
         nc.scalar.square(warm[:], minus_half[:, 0:1])
+        warm_pow = const.tile([P, 1], F32)
+        nc.gpsimd.memset(warm_pow[:], 1.0)
+        nc.gpsimd.tensor_scalar_max(out=warm_pow[:], in0=warm_pow[:], scalar1=RMS_EPS * RMS_EPS)
+        nc.gpsimd.tensor_tensor(out=warm_pow[:], in0=warm_pow[:], in1=minus_half[:, 0:1], op=ALU.pow)
 
         gamma_row = const.tile([P, DIM], BF16)
         nc.vector.memset(gamma_row[:], 0.0)
@@ -223,12 +226,16 @@ def tile_ringattention_pa_kernel(tc, x, gamma, w_qkv, out_0, out_1, out_2):
         stage = {}
         deferred = []
 
-        def store(engine, c, tiles):
-            h0 = (c % CHUNKS_PER_TENSOR) * CHUNK_HEADS
+        def store(engine, c, h, tiles):
             engine.dma_start(
-                out=out_views[c // CHUNKS_PER_TENSOR][:, h0 : h0 + CHUNK_HEADS, tiles, :],
-                in_=stage[c][:, :, tiles, :],
+                out=out_views[c // CHUNKS_PER_TENSOR][:, (c % CHUNKS_PER_TENSOR) * CHUNK_HEADS + h, tiles, :],
+                in_=stage[c][:, h, tiles, :],
             )
+
+        def flush():
+            for c, h, tiles in deferred:
+                store(nc.scalar, c, h, tiles)
+            deferred.clear()
 
         def evacuate(c, a):
             if a == 0:
@@ -252,14 +259,13 @@ def tile_ringattention_pa_kernel(tc, x, gamma, w_qkv, out_0, out_1, out_2):
             pairs_per_store = PAIRS // 2 if in_halves else PAIRS
             if (a + 1) % pairs_per_store == 0:
                 tiles = slice(PAIR * (a + 1 - pairs_per_store), PAIR * (a + 1))
-                if c % 2 == 0 and not in_halves:
-                    deferred.append((c, tiles))
-                else:
-                    store(nc.sync, c, tiles)
-            if a == 0:
-                for d, tiles in deferred:
-                    store(nc.scalar, d, tiles)
-                deferred.clear()
+                store(nc.sync, c, 0, tiles)
+                due = (c, 1, tiles)
+            else:
+                due = None
+            flush()
+            if due is not None:
+                deferred.append(due)
 
         regroup_w(0)
         quantise_w(0)
@@ -299,3 +305,4 @@ def tile_ringattention_pa_kernel(tc, x, gamma, w_qkv, out_0, out_1, out_2):
             for a in range(PAIRS):
                 project(c, a)
                 evacuate(c, a)
+        flush()

@@ -226,16 +226,12 @@ def tile_ringattention_pa_kernel(tc, x, gamma, w_qkv, out_0, out_1, out_2):
         stage = {}
         deferred = []
 
-        def store(engine, c, h, tiles):
+        def store(engine, c, tiles):
+            h0 = (c % CHUNKS_PER_TENSOR) * CHUNK_HEADS
             engine.dma_start(
-                out=out_views[c // CHUNKS_PER_TENSOR][:, (c % CHUNKS_PER_TENSOR) * CHUNK_HEADS + h, tiles, :],
-                in_=stage[c][:, h, tiles, :],
+                out=out_views[c // CHUNKS_PER_TENSOR][:, h0 : h0 + CHUNK_HEADS, tiles, :],
+                in_=stage[c][:, :, tiles, :],
             )
-
-        def flush():
-            for c, h, tiles in deferred:
-                store(nc.scalar, c, h, tiles)
-            deferred.clear()
 
         def evacuate(c, a):
             if a == 0:
@@ -259,13 +255,14 @@ def tile_ringattention_pa_kernel(tc, x, gamma, w_qkv, out_0, out_1, out_2):
             pairs_per_store = PAIRS // 2 if in_halves else PAIRS
             if (a + 1) % pairs_per_store == 0:
                 tiles = slice(PAIR * (a + 1 - pairs_per_store), PAIR * (a + 1))
-                store(nc.sync, c, 0, tiles)
-                due = (c, 1, tiles)
-            else:
-                due = None
-            flush()
-            if due is not None:
-                deferred.append(due)
+                if c % 2 == 0 and not in_halves:
+                    deferred.append((c, tiles))
+                else:
+                    store(nc.sync, c, tiles)
+            if a == 0:
+                for d, tiles in deferred:
+                    store(nc.scalar, d, tiles)
+                deferred.clear()
 
         regroup_w(0)
         quantise_w(0)
@@ -305,4 +302,3 @@ def tile_ringattention_pa_kernel(tc, x, gamma, w_qkv, out_0, out_1, out_2):
             for a in range(PAIRS):
                 project(c, a)
                 evacuate(c, a)
-        flush()

@@ -35,7 +35,6 @@ VECTOR_EVERY = 16
 RMS_AHEAD = 3
 NORM_AHEAD = 2
 EARLY_CHUNKS = 2
-HALVED_CHUNKS = 4
 ROOT_DIM = 32.0
 assert ROOT_DIM * ROOT_DIM == DIM
 PSUM_BANKS = 8
@@ -251,15 +250,14 @@ def tile_ringattention_pa_kernel(tc, x, gamma, w_qkv, out_0, out_1, out_2):
                     nc.scalar.mul(dst, src, HEAD_DIM**-0.5)
                 else:
                     nc.scalar.copy(out=dst, in_=src)
-            in_halves = c < HALVED_CHUNKS
-            pairs_per_store = PAIRS // 2 if in_halves else PAIRS
+            pairs_per_store = PAIRS // 2
             if (a + 1) % pairs_per_store == 0:
                 tiles = slice(PAIR * (a + 1 - pairs_per_store), PAIR * (a + 1))
-                if c % 2 == 0 and not in_halves:
+                if a == pairs_per_store - 1 and c >= EARLY_CHUNKS:
                     deferred.append((c, tiles))
                 else:
                     store(nc.sync, c, tiles)
-            if a == 0:
+            if a == pairs_per_store:
                 for d, tiles in deferred:
                     store(nc.scalar, d, tiles)
                 deferred.clear()

from contextlib import ExitStack

import concourse.mybir as mybir
from concourse.masks import make_identity

F32 = mybir.dt.float32
BF16 = mybir.dt.bfloat16
U32 = mybir.dt.uint32
U8 = mybir.dt.uint8
FP8X4 = mybir.dt.float8_e4m3fn_x4
ACT = mybir.ActivationFunctionType
ALU = mybir.AluOpType

P = 128
TOKENS = 1024
DIM = 1024
HEADS = 8
HEAD_DIM = 128
TENSORS = 3
RMS_EPS = 1e-12

PACK = 4
HALF_PACK = PACK // 2
PASSES = DIM // (P * PACK)
TILES = TOKENS // P
PAIR = 2
PAIRS = TILES // PAIR
CHUNK_HEADS = 2
CHUNK = CHUNK_HEADS * HEAD_DIM
TENSOR_COLS = HEADS * HEAD_DIM
CHUNKS_PER_TENSOR = TENSOR_COLS // CHUNK
CHUNKS = TENSORS * CHUNKS_PER_TENSOR
BANK = 512
VECTOR_EVERY = 16
RMS_AHEAD = 3
NORM_AHEAD = 2
EARLY_CHUNKS = 2
ROOT_DIM = 32.0
assert ROOT_DIM * ROOT_DIM == DIM
PSUM_BANKS = 8

FLOPS = 2 * TOKENS * DIM * TENSORS * TENSOR_COLS


def tile_ringattention_pa_kernel(tc, x, gamma, w_qkv, out_0, out_1, out_2):
    nc = tc.nc

    x_view = x.rearrange("b (p t) k -> p (b t) k", t=TILES)
    out_views = [o.rearrange("b h (p t) d -> p (b h) t d", t=TILES) for o in (out_0, out_1, out_2)]
    w_view = w_qkv.rearrange("(g p j) n -> g p j n", g=PASSES, j=PACK)

    with ExitStack() as ctx:
        const = ctx.enter_context(tc.tile_pool(name="const", bufs=1))
        keep = ctx.enter_context(tc.tile_pool(name="keep", bufs=1))
        work = ctx.enter_context(tc.tile_pool(name="work", bufs=3))
        stages = ctx.enter_context(tc.tile_pool(name="stages", bufs=4))
        psum_gamma = ctx.enter_context(tc.psum_pool(name="psum_gamma", bufs=1))
        psum = ctx.enter_context(tc.psum_pool(name="psum", bufs=PSUM_BANKS - 1))
        ctx.enter_context(tc.manual_schedule())

        gamma_in = const.tile([1, DIM], BF16)
        nc.scalar.dma_start(out=gamma_in[:], in_=gamma.rearrange("(o k) -> o k", o=1))

        x_sb = keep.tile([P, TILES, DIM], BF16)

        def load_x(a):
            tiles = slice(PAIR * a, PAIR * (a + 1))
            nc.sync.dma_start(out=x_sb[:, tiles, :], in_=x_view[:, tiles, :])

        w_raw = {}

        def load_w(first, chunks):
            cols = chunks * CHUNK
            raw = keep.tile([P, PASSES, PACK, cols], BF16, name="w_raw%d" % first)
            for g in range(PASSES):
                nc.sync.dma_start(
                    out=raw[:, g, :, :], in_=w_view[g, :, :, first * CHUNK : first * CHUNK + cols]
                )
            for c in range(chunks):
                w_raw[first + c] = (raw, c * CHUNK)

        load_x(0)
        load_w(0, 1)
        for a in range(1, RMS_AHEAD):
            load_x(a)
        load_w(1, 2)
        for a in range(RMS_AHEAD, PAIRS):
            load_x(a)
        load_w(3, CHUNKS - 3)

        ident = const.tile([P, P], F32)
        make_identity(nc, ident[:])
        spreader = const.tile([P, P], BF16)
        nc.vector.memset(spreader[:], ROOT_DIM)
        minus_half = const.tile([P, TILES], F32)
        nc.vector.memset(minus_half[:], -0.5)
        warm = const.tile([P, 1], F32)
        nc.scalar.square(warm[:], minus_half[:, 0:1])
        warm_pow = const.tile([P, 1], F32)
        nc.gpsimd.memset(warm_pow[:], 1.0)
        nc.gpsimd.tensor_scalar_max(out=warm_pow[:], in0=warm_pow[:], scalar1=RMS_EPS * RMS_EPS)
        nc.gpsimd.tensor_tensor(out=warm_pow[:], in0=warm_pow[:], in1=minus_half[:, 0:1], op=ALU.pow)

        gamma_row = const.tile([P, DIM], BF16)
        nc.vector.memset(gamma_row[:], 0.0)
        nc.vector.tensor_copy(out=gamma_row[0:1, :], in_=gamma_in[:])
        gamma_b = psum_gamma.tile([P, DIM], BF16)
        for half in range(DIM // BANK):
            cols = slice(half * BANK, (half + 1) * BANK)
            nc.tensor.matmul(
                out=gamma_b[:, cols], lhsT=spreader[:], rhs=gamma_row[:, cols], start=True, stop=True
            )

        x_codes = keep.tile([P, TILES, PASSES * P], U32, align_bytes=64)
        x_scales = keep.tile([P, TILES, PASSES * P], U8, align_bytes=64)
        w_codes = keep.tile([P, CHUNKS, PASSES * CHUNK], U32, align_bytes=64)
        w_scales = keep.tile([P, CHUNKS, PASSES * CHUNK], U8, align_bytes=64)

        sum_sq = keep.tile([P, TILES], F32)
        sum_sq_clamped = keep.tile([P, TILES], F32)
        inv_l2 = keep.tile([P, TILES], F32)
        turned = {}
        x_grouped = {}

        def inverse_norm(a):
            for t in range(PAIR * a, PAIR * (a + 1)):
                squares = work.tile([P, DIM], BF16)
                nc.scalar.activation(
                    out=squares[:], in_=x_sb[:, t, :], func=ACT.Square, accum_out=sum_sq[:, t : t + 1]
                )
                nc.gpsimd.tensor_scalar_max(
                    out=sum_sq_clamped[:, t : t + 1], in0=sum_sq[:, t : t + 1], scalar1=RMS_EPS * RMS_EPS
                )
                nc.gpsimd.tensor_tensor(
                    out=inv_l2[:, t : t + 1], in0=sum_sq_clamped[:, t : t + 1], in1=minus_half[:, t : t + 1], op=ALU.pow
                )

        def normalise(a):
            for t in range(PAIR * a, PAIR * (a + 1)):
                normed = work.tile([P, DIM], BF16)
                nc.vector.scalar_tensor_tensor(
                    out=normed[:],
                    in0=x_sb[:, t, :],
                    scalar=inv_l2[:, t : t + 1],
                    in1=gamma_b[:],
                    op0=ALU.mult,
                    op1=ALU.mult,
                )
                normed_words = normed[:].bitcast(F32).rearrange(
                    "m (g p u) -> m g u p", g=PASSES, u=HALF_PACK
                )
                turned[t] = psum.tile([P, PASSES, HALF_PACK, P], F32, name="turned", tag="bank")
                for g in range(PASSES):
                    for u in range(HALF_PACK):
                        nc.tensor.transpose(turned[t][:, g, u, :], normed_words[:, g, u, :], ident[:])

        def regroup_x(a):
            x_grouped[a] = work.tile([P, PAIR, DIM], BF16, name="x_grouped", align_bytes=64)
            for i in range(PAIR):
                nc.scalar.copy(
                    out=x_grouped[a][:, i, :].bitcast(F32).rearrange(
                        "p (g m u) -> p g m u", g=PASSES, u=HALF_PACK
                    ),
                    in_=turned[PAIR * a + i][:].rearrange("p g u m -> p g m u"),
                )

        def quantise_x(a):
            if a == PAIRS - 1:
                for i in range(PAIR):
                    nc.vector.quantize_mx(
                        out=x_codes[:, PAIR * a + i, :].bitcast(FP8X4),
                        scales=x_scales[:, PAIR * a + i, :],
                        in_=x_grouped[a][:, i, :],
                    )
                return
            tiles = slice(PAIR * a, PAIR * (a + 1))
            nc.vector.quantize_mx(
                out=x_codes[:, tiles, :].rearrange("p t w -> p (t w)").bitcast(FP8X4),
                scales=x_scales[:, tiles, :].rearrange("p t w -> p (t w)"),
                in_=x_grouped[a][:].rearrange("p t k -> p (t k)"),
            )

        w_grouped = {}

        def regroup_w(c, passes=PASSES):
            raw, lo = w_raw[c]
            w_grouped[c] = work.tile([P, PASSES, CHUNK, PACK], BF16, name="w_grouped", align_bytes=64)
            for g in range(passes):
                nc.vector.tensor_copy(
                    out=w_grouped[c][:, g, :, :].rearrange("p (c i) j -> p c j i", i=4),
                    in_=raw[:, g, :, lo : lo + CHUNK].rearrange("p j (c i) -> p c j i", i=4),
                )

        def regroup_w_on_scalar(c, g):
            raw, lo = w_raw[c]
            nc.scalar.copy(
                out=w_grouped[c][:, g, :, :],
                in_=raw[:, g, :, lo : lo + CHUNK].rearrange("p j n -> p n j"),
            )

        def quantise_w(c):
            nc.vector.quantize_mx(
                out=w_codes[:, c, :].bitcast(FP8X4),
                scales=w_scales[:, c, :],
                in_=w_grouped[c][:].rearrange("p g n j -> p (g n j)"),
            )

        acc = {}

        def project(c, a):
            acc[c, a] = psum.tile([P, PAIR, CHUNK], F32, name="acc", tag="bank")
            for i in range(PAIR):
                t = PAIR * a + i
                for g in range(PASSES):
                    nc.tensor.matmul_mx(
                        out=acc[c, a][:, i, :],
                        lhsT=x_codes[:, t, g * P : (g + 1) * P].bitcast(FP8X4),
                        lhsT_scale=x_scales[:, t, g * P : (g + 1) * P],
                        rhs=w_codes[:, c, g * CHUNK : (g + 1) * CHUNK].bitcast(FP8X4),
                        rhs_scale=w_scales[:, c, g * CHUNK : (g + 1) * CHUNK],
                        start=(g == 0),
                        stop=(g == PASSES - 1),
                    )

        stage = {}
        deferred = []

        def store(engine, c, tiles):
            h0 = (c % CHUNKS_PER_TENSOR) * CHUNK_HEADS
            engine.dma_start(
                out=out_views[c // CHUNKS_PER_TENSOR][:, h0 : h0 + CHUNK_HEADS, tiles, :],
                in_=stage[c][:, :, tiles, :],
            )

        def evacuate(c, a):
            if a == 0:
                stage[c] = stages.tile([P, CHUNK_HEADS, TILES, HEAD_DIM], F32, name="stage")
            dst = stage[c][:, :, PAIR * a : PAIR * (a + 1), :]
            src = acc[c, a][:].rearrange("p i (h d) -> p h i d", h=CHUNK_HEADS)
            is_q = c < CHUNKS_PER_TENSOR
            if (c * PAIRS + a) % VECTOR_EVERY == VECTOR_EVERY - 1:
                if is_q:
                    nc.vector.tensor_scalar(
                        out=dst, in0=src, scalar1=HEAD_DIM**-0.5, scalar2=None, op0=ALU.mult
                    )
                else:
                    nc.vector.tensor_copy(out=dst, in_=src)
            else:
                if is_q:
                    nc.scalar.mul(dst, src, HEAD_DIM**-0.5)
                else:
                    nc.scalar.copy(out=dst, in_=src)
            pairs_per_store = PAIRS // 2
            if (a + 1) % pairs_per_store == 0:
                tiles = slice(PAIR * (a + 1 - pairs_per_store), PAIR * (a + 1))
                if a == pairs_per_store - 1 and c >= EARLY_CHUNKS:
                    deferred.append((c, tiles))
                else:
                    store(nc.sync, c, tiles)
            if a == pairs_per_store:
                for d, tiles in deferred:
                    store(nc.scalar, d, tiles)
                deferred.clear()

        regroup_w(0)
        quantise_w(0)
        for a in range(RMS_AHEAD):
            inverse_norm(a)
        for a in range(NORM_AHEAD):
            normalise(a)
        regroup_w(1)
        filled = []
        for a in range(PAIRS):
            regroup_x(a)
            if a + RMS_AHEAD < PAIRS:
                inverse_norm(a + RMS_AHEAD)
            for c, b in filled[:a]:
                evacuate(c, b)
            filled = filled[a:]
            quantise_x(a)
            if a == 0:
                quantise_w(1)
            if a == PAIRS - 2:
                regroup_w(2)
            for c in range(EARLY_CHUNKS):
                project(c, a)
                filled.append((c, a))
            if a + NORM_AHEAD < PAIRS:
                normalise(a + NORM_AHEAD)
        quantise_w(2)
        regroup_w(3)
        for c, b in filled:
            evacuate(c, b)

        for c in range(EARLY_CHUNKS, CHUNKS):
            if c + 1 < CHUNKS:
                quantise_w(c + 1)
            if c + 2 < CHUNKS:
                regroup_w(c + 2)
            for a in range(PAIRS):
                project(c, a)
                evacuate(c, a)
